import numpy as np
import ml_dtypes


def mxq(x, axis, fmt="e4m3"):
    dtype, down = {"e4m3": (ml_dtypes.float8_e4m3fn, 7), "e5m2": (ml_dtypes.float8_e5m2, 14)}[fmt]
    v = np.moveaxis(np.asarray(x, np.float32).astype(ml_dtypes.bfloat16).astype(np.float64), axis, -1)
    blocks = v.reshape(v.shape[:-1] + (-1, 32))
    amax = np.abs(blocks).max(-1, keepdims=True)
    byte = np.maximum(np.where(amax > 0, np.frexp(amax)[1] - 1 + 127, 0) - down, 1)
    scale = np.exp2(byte - 127.0)
    codes = (blocks / scale).astype(np.float32).astype(dtype).astype(np.float64)
    return np.moveaxis((codes * scale).reshape(v.shape), -1, axis)


WIDE = False


def mx_kscale(k):
    if not WIDE:
        return np.ones(k)
    levels = np.array([10, -10, 5, -5, 0])
    a = np.random.permutation(np.resize(levels, k // 512 * 4)).reshape(k // 512, 4)
    idx = np.arange(k)
    return np.exp2(a[idx // 512, idx % 128 // 32])


BF16 = ml_dtypes.bfloat16


def bf(x):
    return np.asarray(x, np.float32).astype(BF16)


def f64(x):
    return np.asarray(x).astype(np.float64)


N, N_CH, X, H = 4096, 4, 512, 256
K = N_CH * H


def sigmoid(v):
    return 1.0 / (1.0 + np.exp(-v))


def setup_inputs():
    s, t = mx_kscale(X), mx_kscale(K)
    return {
        "x": bf(np.random.standard_normal((N, X)) * s),
        "x_mask": bf(np.random.random(N) < 0.75),
        "neighbour_h": bf(np.random.standard_normal((N, N_CH, H)) * t.reshape(N_CH, H)),
        "neighbour_c": bf(np.random.standard_normal((N, N_CH, H))),
        "W_f_in": bf(np.random.standard_normal((X, H)) * 0.5 / np.sqrt(X) / s[:, None]),
        "b_f_in": bf(np.random.standard_normal(H) * 0.3),
        "W_aggr_f": bf(np.random.standard_normal((K, K)) / np.sqrt(K) / t[:, None]),
        "b_aggr_f": bf(np.random.standard_normal(K) * 0.3),
    }


def reference(x, x_mask, neighbour_h, neighbour_c, W_f_in, b_f_in, W_aggr_f, b_aggr_f):
    h_flat = f64(neighbour_h).reshape(N, K)
    f_input = ((mxq(f64(x), 1, "e4m3") @ mxq(f64(W_f_in), 0, "e4m3")) + f64(b_f_in)) * f64(x_mask)[:, None]
    f_input = np.tile(f_input, (1, N_CH))
    f_gate = (mxq(h_flat, 1, "e4m3") @ mxq(f64(W_aggr_f), 0, "e4m3")) + f64(b_aggr_f) + f_input
    f_aggr = f_gate + f_input
    f = sigmoid(f_aggr).reshape(N, N_CH, H)
    return np.sum(f * f64(neighbour_c), axis=1)

@@ -1,0 +1,285 @@
+from contextlib import ExitStack
+
+import concourse.mybir as mybir
+from concourse.masks import make_identity
+
+F32 = mybir.dt.float32
+BF16 = mybir.dt.bfloat16
+U32 = mybir.dt.uint32
+U8 = mybir.dt.uint8
+FP8X4 = mybir.dt.float8_e4m3fn_x4
+AF = mybir.ActivationFunctionType
+ALU = mybir.AluOpType
+
+P = 128
+NODES = 4096
+XDIM = 512
+HDIM = 256
+KIDS = 4
+KDIM = KIDS * HDIM
+CHUNK = 512
+TILES = CHUNK // P
+NCHUNK = NODES // CHUNK
+FLOPS = 2 * NODES * KDIM * KDIM + 2 * NODES * XDIM * HDIM
+
+
+def tile_treelstmcell_pa_t_kernel(
+    tc, x, x_mask, neighbour_h, neighbour_c, W_f_in, b_f_in, W_aggr_f, b_aggr_f, out
+):
+    nc = tc.nc
+    x_v = x.rearrange("(c p t) k -> c p (t k)", p=P, t=TILES)
+    h_v = neighbour_h.rearrange("(c p t) k j -> c p (t k j)", p=P, t=TILES)
+    c_v = neighbour_c.rearrange("(c p t) k j -> c p (t k j)", p=P, t=TILES)
+    o_v = out.rearrange("(c p t) j -> c p (t j)", p=P, t=TILES)
+    w_v = W_aggr_f.rearrange("(s q e) c -> s q (e c)", s=4, q=P, e=2)
+    wf_v = W_f_in.rearrange("(u q e) c -> q u (e c)", u=2, q=P, e=2)
+
+    with ExitStack() as ctx:
+        const = ctx.enter_context(tc.tile_pool(name="const", bufs=1))
+        loads = ctx.enter_context(tc.tile_pool(name="loads", bufs=3))
+        quant = ctx.enter_context(tc.tile_pool(name="quant", bufs=2))
+        work = ctx.enter_context(tc.tile_pool(name="work", bufs=2))
+        zps = ctx.enter_context(tc.psum_pool(name="zps", bufs=4))
+        fps = ctx.enter_context(tc.psum_pool(name="fps", bufs=2))
+        tps = ctx.enter_context(tc.psum_pool(name="tps", bufs=2))
+
+        xs = {}
+        hs = {}
+        cs = {}
+        ms = {}
+
+        def load_xh(c):
+            x_sb = loads.tile([P, TILES * XDIM], BF16, tag="x")
+            nc.sync.dma_start(out=x_sb[:], in_=x_v[c])
+            xs[c] = x_sb
+            m_sb = loads.tile([P, CHUNK], BF16, tag="m")
+            nc.sync.dma_start(
+                out=m_sb[:], in_=x_mask[c * CHUNK : (c + 1) * CHUNK].partition_broadcast(P)
+            )
+            ms[c] = m_sb
+            h_sb = loads.tile([P, TILES * KDIM], BF16, tag="h")
+            nc.sync.dma_start(out=h_sb[:], in_=h_v[c])
+            hs[c] = h_sb
+
+        def load_c(c):
+            c_sb = loads.tile([P, TILES * KDIM], BF16, tag="c")
+            nc.sync.dma_start(out=c_sb[:], in_=c_v[c])
+            cs[c] = c_sb
+
+        bias_rows = const.tile([P, P], BF16)
+        nc.vector.memset(bias_rows[:], 0.0)
+        nc.scalar.dma_start(out=bias_rows[0:8, :], in_=b_aggr_f.rearrange("(r q) -> r q", q=P))
+        nc.scalar.dma_start(out=bias_rows[8:10, :], in_=b_f_in.rearrange("(r q) -> r q", q=P))
+
+        wf_raw = const.tile([P, 4, HDIM], BF16)
+        nc.sync.dma_start(out=wf_raw[:].rearrange("q (u e) c -> q u (e c)", u=2), in_=wf_v)
+        load_xh(0)
+        w_raw = const.tile([P, 8, KDIM], BF16)
+        for s in range(4):
+            nc.sync.dma_start(
+                out=w_raw[:, 2 * s : 2 * s + 2, :].rearrange("q e c -> q (e c)"), in_=w_v[s]
+            )
+        load_c(0)
+        load_xh(1)
+        load_c(1)
+
+        ident = const.tile([P, P], F32)
+        make_identity(nc, ident[:])
+        ident_bf = const.tile([P, P], BF16)
+        make_identity(nc, ident_bf[:])
+
+        bias_ps = tps.tile([P, P], BF16, tag="tp")
+        nc.tensor.transpose(bias_ps[:], bias_rows[:], ident_bf[:])
+        bias = const.tile([P, 16], F32)
+        nc.vector.tensor_copy(out=bias[:, 0:10], in_=bias_ps[:, 0:10])
+        bf2 = const.tile([P, 2], F32)
+        nc.vector.tensor_scalar_mul(out=bf2[:], in0=bias[:, 8:10], scalar1=2.0)
+
+        wf_grp = const.tile([P, HDIM, 4], BF16, align_bytes=64)
+        wf_codes = const.tile([P, HDIM], U32, align_bytes=64)
+        wf_scl = const.tile([P, HDIM], U8, align_bytes=64)
+        nc.vector.tensor_copy(out=wf_grp[:], in_=wf_raw[:].rearrange("q t c -> q c t"))
+
+        w_grp = const.tile([P, 2, KDIM, 4], BF16, align_bytes=64)
+        w_codes = const.tile([P, 2, KDIM], U32, align_bytes=64)
+        w_scl = const.tile([P, 2, KDIM], U8, align_bytes=64)
+
+        def w_regroup(g, cb, eng):
+            cols = slice(cb * HDIM, (cb + 1) * HDIM)
+            src = w_raw[:, 4 * g : 4 * g + 4, cols].rearrange("q t c -> q c t")
+            if eng == 0:
+                nc.vector.tensor_copy(out=w_grp[:, g, cols, :], in_=src)
+            else:
+                nc.scalar.copy(out=w_grp[:, g, cols, :], in_=src)
+
+        def w_quant(g, cb):
+            cols = slice(cb * HDIM, (cb + 1) * HDIM)
+            nc.vector.quantize_mx(
+                out=w_codes[:, g, cols].bitcast(FP8X4),
+                scales=w_scl[:, g, cols],
+                in_=w_grp[:, g, cols, :].rearrange("q c t -> q (c t)"),
+            )
+
+        grps = {}
+        codes = {}
+
+        def tr_unit(c, op, hh):
+            if op == 0:
+                words = xs[c][:].bitcast(F32)
+                wpt = XDIM // 2
+                g = 0
+            else:
+                words = hs[c][:].bitcast(F32)
+                wpt = KDIM // 2
+                g = op - 1
+            if hh == 0:
+                grp = quant.tile([P, CHUNK * 4], BF16, tag="grp%d" % op, align_bytes=64)
+                grps[(c, op)] = grp
+            grp = grps[(c, op)]
+            tp = tps.tile([P, 2, 2 * P], F32, tag="tp")
+            for u in range(2):
+                for tt in range(2):
+                    col = (2 * hh + tt) * wpt + (2 * g + u) * P
+                    nc.tensor.transpose(
+                        tp[:, u, tt * P : (tt + 1) * P], words[:, col : col + P], ident[:]
+                    )
+            dst = grp[:].bitcast(F32).rearrange("p (n u) -> p n u", u=2)
+            nc.scalar.copy(
+                out=dst[:, hh * 2 * P : (hh + 1) * 2 * P, :], in_=tp[:].rearrange("p u n -> p n u")
+            )
+
+        def tr_quant(c, op):
+            cd = quant.tile([P, CHUNK], U32, tag="cd%d" % op, align_bytes=64)
+            sc = quant.tile([P, CHUNK], U8, tag="sc%d" % op, align_bytes=64)
+            nc.vector.quantize_mx(out=cd[:].bitcast(FP8X4), scales=sc[:], in_=grps[(c, op)][:])
+            codes[(c, op)] = (cd, sc)
+
+        gts = {}
+
+        def fi_stage(c):
+            cd, sc = codes[(c, 0)]
+            for jt in range(2):
+                cols = slice(jt * P, (jt + 1) * P)
+                fz = zps.tile([P, CHUNK], F32, tag="z")
+                nc.tensor.matmul_mx(
+                    out=fz[:],
+                    lhsT=wf_codes[:, cols].bitcast(FP8X4),
+                    lhsT_scale=wf_scl[:, cols],
+                    rhs=cd[:].bitcast(FP8X4),
+                    rhs_scale=sc[:],
+                    start=True,
+                    stop=True,
+                )
+                y2 = work.tile([P, CHUNK], F32, tag="y%d" % jt)
+                nc.scalar.activation(
+                    out=y2[:], in_=fz[:], func=AF.Identity, bias=bf2[:, jt : jt + 1], scale=2.0
+                )
+                gt = work.tile([P, CHUNK], F32, tag="g%d" % jt)
+                nc.gpsimd.tensor_tensor(
+                    out=gt[:].rearrange("q (t p) -> q t p", t=TILES),
+                    in0=y2[:].rearrange("q (t p) -> q t p", t=TILES),
+                    in1=ms[c][:].rearrange("q (p t) -> q t p", t=TILES),
+                    op=ALU.mult,
+                )
+                gts[(c, jt)] = gt
+
+        fts = {}
+
+        def z_step(c, k):
+            for jt in range(2):
+                ct = 2 * k + jt
+                cols = slice(ct * P, (ct + 1) * P)
+                zp = zps.tile([P, CHUNK], F32, tag="z")
+                for g in range(2):
+                    cd, sc = codes[(c, 1 + g)]
+                    nc.tensor.matmul_mx(
+                        out=zp[:],
+                        lhsT=w_codes[:, g, cols].bitcast(FP8X4),
+                        lhsT_scale=w_scl[:, g, cols],
+                        rhs=cd[:].bitcast(FP8X4),
+                        rhs_scale=sc[:],
+                        start=(g == 0),
+                        stop=(g == 1),
+                    )
+                u_sb = work.tile([P, CHUNK], F32, tag="u", bufs=4)
+                nc.vector.tensor_tensor(out=u_sb[:], in0=zp[:], in1=gts[(c, jt)][:], op=ALU.add)
+                f_sb = work.tile([P, CHUNK], F32, tag="f", bufs=6)
+                nc.scalar.activation(
+                    out=f_sb[:], in_=u_sb[:], func=AF.Sigmoid, bias=bias[:, ct : ct + 1], scale=1.0
+                )
+                fts[(c, ct)] = f_sb
+
+        prods = {}
+        accs = {}
+
+        def fb_step(c, k):
+            c4 = cs[c][:].rearrange("p (t k j) -> p t k j", t=TILES, k=KIDS)
+            prod = work.tile([P, TILES, HDIM], F32, tag="prod", bufs=3)
+            for hh in range(2):
+                fb = fps.tile([P, 2, HDIM], F32, tag="fb")
+                for tt in range(2):
+                    t = 2 * hh + tt
+                    for jt in range(2):
+                        nc.tensor.transpose(
+                            fb[:, tt, jt * P : (jt + 1) * P],
+                            fts[(c, 2 * k + jt)][:, t * P : (t + 1) * P],
+                            ident[:],
+                        )
+                nc.vector.tensor_tensor(
+                    out=prod[:, 2 * hh : 2 * hh + 2, :],
+                    in0=fb[:],
+                    in1=c4[:, 2 * hh : 2 * hh + 2, k, :],
+                    op=ALU.mult,
+                )
+            if k == 0:
+                prods[c] = prod
+            elif k == 1:
+                acc = work.tile([P, TILES, HDIM], F32, tag="acc")
+                nc.gpsimd.tensor_tensor(out=acc[:], in0=prods[c][:], in1=prod[:], op=ALU.add)
+                accs[c] = acc
+            else:
+                nc.gpsimd.tensor_tensor(out=accs[c][:], in0=accs[c][:], in1=prod[:], op=ALU.add)
+            if k == KIDS - 1:
+                nc.gpsimd.dma_start(out=o_v[c], in_=accs[c][:].rearrange("p t j -> p (t j)"))
+
+        for op in range(3):
+            tr_unit(0, op, 0)
+            tr_unit(0, op, 1)
+        nc.vector.quantize_mx(
+            out=wf_codes[:].bitcast(FP8X4),
+            scales=wf_scl[:],
+            in_=wf_grp[:].rearrange("q c t -> q (c t)"),
+        )
+        tr_quant(0, 0)
+        w_regroup(0, 0, 0)
+        w_regroup(1, 0, 0)
+        tr_quant(0, 1)
+        tr_quant(0, 2)
+        fi_stage(0)
+        w_quant(0, 0)
+        w_quant(1, 0)
+        for cb in range(1, 4):
+            w_regroup(0, cb, 0)
+            w_regroup(1, cb, 1)
+        for cb in range(1, 4):
+            w_quant(0, cb)
+            w_quant(1, cb)
+
+        steps = [(c, k) for c in range(NCHUNK) for k in range(KIDS)]
+        for s, (c, k) in enumerate(steps):
+            z_step(c, k)
+            if c + 1 < NCHUNK:
+                if k >= 1:
+                    tr_quant(c + 1, k - 1)
+                if k == 0 and c + 2 < NCHUNK:
+                    load_xh(c + 2)
+                if k < 3:
+                    tr_unit(c + 1, k, 0)
+                    tr_unit(c + 1, k, 1)
+                if k == 3:
+                    fi_stage(c + 1)
+            if s >= 1:
+                fb_step(steps[s - 1][0], steps[s - 1][1])
+            if k == 0 and c + 2 < NCHUNK:
+                load_c(c + 2)
+        fb_step(NCHUNK - 1, KIDS - 1)

@@ -31,7 +31,7 @@ def tile_treelstmcell_pa_t_kernel(
     h_v = neighbour_h.rearrange("(c p t) k j -> c p (t k j)", p=P, t=TILES)
     c_v = neighbour_c.rearrange("(c p t) k j -> c p (t k j)", p=P, t=TILES)
     o_v = out.rearrange("(c p t) j -> c p (t j)", p=P, t=TILES)
-    w_v = W_aggr_f.rearrange("(s q e) c -> s q (e c)", s=4, q=P, e=2)
+    w_v = W_aggr_f.rearrange("(s q e) c -> s q e c", s=4, q=P, e=2)
     wf_v = W_f_in.rearrange("(u q e) c -> q u (e c)", u=2, q=P, e=2)
 
     with ExitStack() as ctx:
@@ -42,6 +42,7 @@ def tile_treelstmcell_pa_t_kernel(
         zps = ctx.enter_context(tc.psum_pool(name="zps", bufs=4))
         fps = ctx.enter_context(tc.psum_pool(name="fps", bufs=2))
         tps = ctx.enter_context(tc.psum_pool(name="tps", bufs=2))
+        ctx.enter_context(tc.manual_schedule())
 
         xs = {}
         hs = {}
@@ -76,8 +77,10 @@ def tile_treelstmcell_pa_t_kernel(
         load_xh(0)
         w_raw = const.tile([P, 8, KDIM], BF16)
         for s in range(4):
+            nc.sync.dma_start(out=w_raw[:, 2 * s : 2 * s + 2, 0:HDIM], in_=w_v[s][:, :, 0:HDIM])
+        for s in range(4):
             nc.sync.dma_start(
-                out=w_raw[:, 2 * s : 2 * s + 2, :].rearrange("q e c -> q (e c)"), in_=w_v[s]
+                out=w_raw[:, 2 * s : 2 * s + 2, HDIM:KDIM], in_=w_v[s][:, :, HDIM:KDIM]
             )
         load_c(0)
         load_xh(1)
@@ -88,12 +91,8 @@ def tile_treelstmcell_pa_t_kernel(
         ident_bf = const.tile([P, P], BF16)
         make_identity(nc, ident_bf[:])
 
-        bias_ps = tps.tile([P, P], BF16, tag="tp")
-        nc.tensor.transpose(bias_ps[:], bias_rows[:], ident_bf[:])
         bias = const.tile([P, 16], F32)
-        nc.vector.tensor_copy(out=bias[:, 0:10], in_=bias_ps[:, 0:10])
         bf2 = const.tile([P, 2], F32)
-        nc.vector.tensor_scalar_mul(out=bf2[:], in0=bias[:, 8:10], scalar1=2.0)
 
         wf_grp = const.tile([P, HDIM, 4], BF16, align_bytes=64)
         wf_codes = const.tile([P, HDIM], U32, align_bytes=64)
@@ -110,7 +109,14 @@ def tile_treelstmcell_pa_t_kernel(
             if eng == 0:
                 nc.vector.tensor_copy(out=w_grp[:, g, cols, :], in_=src)
             else:
-                nc.scalar.copy(out=w_grp[:, g, cols, :], in_=src)
+                nc.gpsimd.tensor_scalar(
+                    out=w_grp[:, g, cols, :],
+                    in0=src,
+                    scalar1=1.0,
+                    scalar2=0.0,
+                    op0=ALU.mult,
+                    op1=ALU.add,
+                )
 
         def w_quant(g, cb):
             cols = slice(cb * HDIM, (cb + 1) * HDIM)
@@ -215,6 +221,7 @@ def tile_treelstmcell_pa_t_kernel(
         def fb_step(c, k):
             c4 = cs[c][:].rearrange("p (t k j) -> p t k j", t=TILES, k=KIDS)
             prod = work.tile([P, TILES, HDIM], F32, tag="prod", bufs=3)
+            last = c == NCHUNK - 1
             for hh in range(2):
                 fb = fps.tile([P, 2, HDIM], F32, tag="fb")
                 for tt in range(2):
@@ -231,43 +238,63 @@ def tile_treelstmcell_pa_t_kernel(
                     in1=c4[:, 2 * hh : 2 * hh + 2, k, :],
                     op=ALU.mult,
                 )
+                if last and k >= 2:
+                    half = slice(2 * hh, 2 * hh + 2)
+                    eng = nc.vector if k == 3 else nc.gpsimd
+                    eng.tensor_tensor(
+                        out=accs[c][:, half, :], in0=accs[c][:, half, :], in1=prod[:, half, :], op=ALU.add
+                    )
+                    if k == 3:
+                        nc.sync.dma_start(
+                            out=o_v[c][:, hh * 2 * HDIM : (hh + 1) * 2 * HDIM],
+                            in_=accs[c][:, half, :].rearrange("p t j -> p (t j)"),
+                        )
             if k == 0:
                 prods[c] = prod
             elif k == 1:
                 acc = work.tile([P, TILES, HDIM], F32, tag="acc")
                 nc.gpsimd.tensor_tensor(out=acc[:], in0=prods[c][:], in1=prod[:], op=ALU.add)
                 accs[c] = acc
-            else:
+            elif not last:
                 nc.gpsimd.tensor_tensor(out=accs[c][:], in0=accs[c][:], in1=prod[:], op=ALU.add)
-            if k == KIDS - 1:
-                nc.gpsimd.dma_start(out=o_v[c], in_=accs[c][:].rearrange("p t j -> p (t j)"))
+                if k == KIDS - 1:
+                    nc.sync.dma_start(out=o_v[c], in_=accs[c][:].rearrange("p t j -> p (t j)"))
 
-        for op in range(3):
-            tr_unit(0, op, 0)
-            tr_unit(0, op, 1)
+        tr_unit(0, 0, 0)
+        tr_unit(0, 0, 1)
         nc.vector.quantize_mx(
             out=wf_codes[:].bitcast(FP8X4),
             scales=wf_scl[:],
             in_=wf_grp[:].rearrange("q c t -> q (c t)"),
         )
+        bias_ps = tps.tile([P, P], BF16, tag="tp")
+        nc.tensor.transpose(bias_ps[:], bias_rows[:], ident_bf[:])
+        nc.vector.tensor_copy(out=bias[:, 0:10], in_=bias_ps[:, 0:10])
+        nc.vector.tensor_scalar_mul(out=bf2[:], in0=bias[:, 8:10], scalar1=2.0)
         tr_quant(0, 0)
+        tr_unit(0, 1, 0)
+        tr_unit(0, 1, 1)
+        fi_stage(0)
+        tr_unit(0, 2, 0)
+        tr_unit(0, 2, 1)
         w_regroup(0, 0, 0)
         w_regroup(1, 0, 0)
         tr_quant(0, 1)
-        tr_quant(0, 2)
-        fi_stage(0)
         w_quant(0, 0)
         w_quant(1, 0)
+        tr_quant(0, 2)
         for cb in range(1, 4):
-            w_regroup(0, cb, 0)
+            w_regroup(0, cb, 1)
             w_regroup(1, cb, 1)
-        for cb in range(1, 4):
-            w_quant(0, cb)
-            w_quant(1, cb)
 
         steps = [(c, k) for c in range(NCHUNK) for k in range(KIDS)]
         for s, (c, k) in enumerate(steps):
+            if k == 3 and c + 1 < NCHUNK:
+                fi_stage(c + 1)
             z_step(c, k)
+            if c == 0 and k < 3:
+                w_quant(0, k + 1)
+                w_quant(1, k + 1)
             if c + 1 < NCHUNK:
                 if k >= 1:
                     tr_quant(c + 1, k - 1)
@@ -276,8 +303,6 @@ def tile_treelstmcell_pa_t_kernel(
                 if k < 3:
                     tr_unit(c + 1, k, 0)
                     tr_unit(c + 1, k, 1)
-                if k == 3:
-                    fi_stage(c + 1)
             if s >= 1:
                 fb_step(steps[s - 1][0], steps[s - 1][1])
             if k == 0 and c + 2 < NCHUNK:

@@ -162,9 +162,9 @@ def tile_treelstmcell_pa_t_kernel(
 
         gts = {}
 
-        def fi_stage(c):
+        def fi_half(c, jt0):
             cd, sc = codes[(c, 0)]
-            for jt in range(2):
+            for jt in range(jt0, jt0 + 1):
                 cols = slice(jt * P, (jt + 1) * P)
                 fz = zps.tile([P, CHUNK], F32, tag="z")
                 nc.tensor.matmul_mx(
@@ -191,8 +191,8 @@ def tile_treelstmcell_pa_t_kernel(
 
         fts = {}
 
-        def z_step(c, k):
-            for jt in range(2):
+        def z_half(c, k, jt0):
+            for jt in range(jt0, jt0 + 1):
                 ct = 2 * k + jt
                 cols = slice(ct * P, (ct + 1) * P)
                 zp = zps.tile([P, CHUNK], F32, tag="z")
@@ -216,13 +216,17 @@ def tile_treelstmcell_pa_t_kernel(
                 fts[(c, ct)] = f_sb
 
         prods = {}
+        cur = [None]
         accs = {}
 
-        def fb_step(c, k):
+        def fb_half(c, k, hh0):
             c4 = cs[c][:].rearrange("p (t k j) -> p t k j", t=TILES, k=KIDS)
-            prod = work.tile([P, TILES, HDIM], F32, tag="prod", bufs=3)
+            if hh0 == 0:
+                prod = work.tile([P, TILES, HDIM], F32, tag="prod", bufs=3)
+                cur[0] = prod
+            prod = cur[0]
             last = c == NCHUNK - 1
-            for hh in range(2):
+            for hh in range(hh0, hh0 + 1):
                 fb = fps.tile([P, 2, HDIM], F32, tag="fb")
                 for tt in range(2):
                     t = 2 * hh + tt
@@ -249,6 +253,8 @@ def tile_treelstmcell_pa_t_kernel(
                             out=o_v[c][:, hh * 2 * HDIM : (hh + 1) * 2 * HDIM],
                             in_=accs[c][:, half, :].rearrange("p t j -> p (t j)"),
                         )
+            if hh0 == 0:
+                return
             if k == 0:
                 prods[c] = prod
             elif k == 1:
@@ -274,7 +280,8 @@ def tile_treelstmcell_pa_t_kernel(
         tr_quant(0, 0)
         tr_unit(0, 1, 0)
         tr_unit(0, 1, 1)
-        fi_stage(0)
+        fi_half(0, 0)
+        fi_half(0, 1)
         tr_unit(0, 2, 0)
         tr_unit(0, 2, 1)
         w_regroup(0, 0, 0)
@@ -289,22 +296,22 @@ def tile_treelstmcell_pa_t_kernel(
 
         steps = [(c, k) for c in range(NCHUNK) for k in range(KIDS)]
         for s, (c, k) in enumerate(steps):
-            if k == 3 and c + 1 < NCHUNK:
-                fi_stage(c + 1)
-            z_step(c, k)
-            if c == 0 and k < 3:
-                w_quant(0, k + 1)
-                w_quant(1, k + 1)
-            if c + 1 < NCHUNK:
-                if k >= 1:
+            more = c + 1 < NCHUNK
+            for half in range(2):
+                if k == 3 and more:
+                    fi_half(c + 1, half)
+                z_half(c, k, half)
+                if c == 0 and k < 3:
+                    w_quant(half, k + 1)
+                if more and k >= 1 and half == 0:
                     tr_quant(c + 1, k - 1)
-                if k == 0 and c + 2 < NCHUNK:
+                if k == 0 and half == 0 and c + 2 < NCHUNK:
                     load_xh(c + 2)
-                if k < 3:
-                    tr_unit(c + 1, k, 0)
-                    tr_unit(c + 1, k, 1)
-            if s >= 1:
-                fb_step(steps[s - 1][0], steps[s - 1][1])
+                if more and k < 3:
+                    tr_unit(c + 1, k, half)
+                if s >= 1:
+                    fb_half(steps[s - 1][0], steps[s - 1][1], half)
             if k == 0 and c + 2 < NCHUNK:
                 load_c(c + 2)
-        fb_step(NCHUNK - 1, KIDS - 1)
+        fb_half(NCHUNK - 1, KIDS - 1, 0)
+        fb_half(NCHUNK - 1, KIDS - 1, 1)

@@ -20,6 +20,7 @@ KDIM = KIDS * HDIM
 CHUNK = 512
 TILES = CHUNK // P
 NCHUNK = NODES // CHUNK
+LAG = 2
 FLOPS = 2 * NODES * KDIM * KDIM + 2 * NODES * XDIM * HDIM
 
 
@@ -43,13 +44,14 @@ def tile_treelstmcell_pa_t_kernel(
         fps = ctx.enter_context(tc.psum_pool(name="fps", bufs=2))
         tps = ctx.enter_context(tc.psum_pool(name="tps", bufs=2))
         ctx.enter_context(tc.manual_schedule())
+        banks = {"z": zps, "fb": fps, "tp": tps}
 
         xs = {}
         hs = {}
         cs = {}
         ms = {}
 
-        def load_xh(c):
+        def load_x(c):
             x_sb = loads.tile([P, TILES * XDIM], BF16, tag="x")
             nc.sync.dma_start(out=x_sb[:], in_=x_v[c])
             xs[c] = x_sb
@@ -58,7 +60,9 @@ def tile_treelstmcell_pa_t_kernel(
                 out=m_sb[:], in_=x_mask[c * CHUNK : (c + 1) * CHUNK].partition_broadcast(P)
             )
             ms[c] = m_sb
-            h_sb = loads.tile([P, TILES * KDIM], BF16, tag="h")
+
+        def load_h(c):
+            h_sb = loads.tile([P, TILES * KDIM], BF16, tag="h", bufs=2)
             nc.sync.dma_start(out=h_sb[:], in_=h_v[c])
             hs[c] = h_sb
 
@@ -72,9 +76,10 @@ def tile_treelstmcell_pa_t_kernel(
         nc.scalar.dma_start(out=bias_rows[0:8, :], in_=b_aggr_f.rearrange("(r q) -> r q", q=P))
         nc.scalar.dma_start(out=bias_rows[8:10, :], in_=b_f_in.rearrange("(r q) -> r q", q=P))
 
+        load_x(0)
         wf_raw = const.tile([P, 4, HDIM], BF16)
         nc.sync.dma_start(out=wf_raw[:].rearrange("q (u e) c -> q u (e c)", u=2), in_=wf_v)
-        load_xh(0)
+        load_h(0)
         w_raw = const.tile([P, 8, KDIM], BF16)
         for s in range(4):
             nc.sync.dma_start(out=w_raw[:, 2 * s : 2 * s + 2, 0:HDIM], in_=w_v[s][:, :, 0:HDIM])
@@ -82,31 +87,30 @@ def tile_treelstmcell_pa_t_kernel(
             nc.sync.dma_start(
                 out=w_raw[:, 2 * s : 2 * s + 2, HDIM:KDIM], in_=w_v[s][:, :, HDIM:KDIM]
             )
+        load_x(1)
+        load_h(1)
         load_c(0)
-        load_xh(1)
+        load_x(2)
         load_c(1)
 
         ident = const.tile([P, P], F32)
         make_identity(nc, ident[:])
         ident_bf = const.tile([P, P], BF16)
         make_identity(nc, ident_bf[:])
-
         bias = const.tile([P, 16], F32)
         bf2 = const.tile([P, 2], F32)
 
         wf_grp = const.tile([P, HDIM, 4], BF16, align_bytes=64)
         wf_codes = const.tile([P, HDIM], U32, align_bytes=64)
         wf_scl = const.tile([P, HDIM], U8, align_bytes=64)
-        nc.vector.tensor_copy(out=wf_grp[:], in_=wf_raw[:].rearrange("q t c -> q c t"))
-
         w_grp = const.tile([P, 2, KDIM, 4], BF16, align_bytes=64)
         w_codes = const.tile([P, 2, KDIM], U32, align_bytes=64)
         w_scl = const.tile([P, 2, KDIM], U8, align_bytes=64)
 
-        def w_regroup(g, cb, eng):
+        def w_regroup(g, cb, on_vector):
             cols = slice(cb * HDIM, (cb + 1) * HDIM)
             src = w_raw[:, 4 * g : 4 * g + 4, cols].rearrange("q t c -> q c t")
-            if eng == 0:
+            if on_vector:
                 nc.vector.tensor_copy(out=w_grp[:, g, cols, :], in_=src)
             else:
                 nc.gpsimd.tensor_scalar(
@@ -128,8 +132,9 @@ def tile_treelstmcell_pa_t_kernel(
 
         grps = {}
         codes = {}
+        tpt = {}
 
-        def tr_unit(c, op, hh):
+        def tr_pe(c, op, hh, bank):
             if op == 0:
                 words = xs[c][:].bitcast(F32)
                 wpt = XDIM // 2
@@ -138,21 +143,26 @@ def tile_treelstmcell_pa_t_kernel(
                 words = hs[c][:].bitcast(F32)
                 wpt = KDIM // 2
                 g = op - 1
-            if hh == 0:
-                grp = quant.tile([P, CHUNK * 4], BF16, tag="grp%d" % op, align_bytes=64)
-                grps[(c, op)] = grp
-            grp = grps[(c, op)]
-            tp = tps.tile([P, 2, 2 * P], F32, tag="tp")
+            tp = banks[bank].tile([P, 2, 2 * P], F32, tag=bank)
             for u in range(2):
                 for tt in range(2):
                     col = (2 * hh + tt) * wpt + (2 * g + u) * P
                     nc.tensor.transpose(
                         tp[:, u, tt * P : (tt + 1) * P], words[:, col : col + P], ident[:]
                     )
-            dst = grp[:].bitcast(F32).rearrange("p (n u) -> p n u", u=2)
-            nc.scalar.copy(
-                out=dst[:, hh * 2 * P : (hh + 1) * 2 * P, :], in_=tp[:].rearrange("p u n -> p n u")
-            )
+            tpt[(c, op, hh)] = tp
+
+        def tr_cp(c, op, hh, on_vector):
+            if hh == 0:
+                grp = quant.tile([P, CHUNK * 4], BF16, tag="grp%d" % op, align_bytes=64)
+                grps[(c, op)] = grp
+            dst = grps[(c, op)][:].bitcast(F32).rearrange("p (n u) -> p n u", u=2)
+            dst = dst[:, hh * 2 * P : (hh + 1) * 2 * P, :]
+            src = tpt[(c, op, hh)][:].rearrange("p u n -> p n u")
+            if on_vector:
+                nc.vector.tensor_copy(out=dst, in_=src)
+            else:
+                nc.scalar.copy(out=dst, in_=src)
 
         def tr_quant(c, op):
             cd = quant.tile([P, CHUNK], U32, tag="cd%d" % op, align_bytes=64)
@@ -160,158 +170,230 @@ def tile_treelstmcell_pa_t_kernel(
             nc.vector.quantize_mx(out=cd[:].bitcast(FP8X4), scales=sc[:], in_=grps[(c, op)][:])
             codes[(c, op)] = (cd, sc)
 
+        fzs = {}
+        ys = {}
         gts = {}
 
-        def fi_half(c, jt0):
+        def fi_pe(c, jt, bank):
             cd, sc = codes[(c, 0)]
-            for jt in range(jt0, jt0 + 1):
-                cols = slice(jt * P, (jt + 1) * P)
-                fz = zps.tile([P, CHUNK], F32, tag="z")
-                nc.tensor.matmul_mx(
-                    out=fz[:],
-                    lhsT=wf_codes[:, cols].bitcast(FP8X4),
-                    lhsT_scale=wf_scl[:, cols],
-                    rhs=cd[:].bitcast(FP8X4),
-                    rhs_scale=sc[:],
-                    start=True,
-                    stop=True,
-                )
-                y2 = work.tile([P, CHUNK], F32, tag="y%d" % jt)
-                nc.scalar.activation(
-                    out=y2[:], in_=fz[:], func=AF.Identity, bias=bf2[:, jt : jt + 1], scale=2.0
-                )
-                gt = work.tile([P, CHUNK], F32, tag="g%d" % jt)
-                nc.gpsimd.tensor_tensor(
-                    out=gt[:].rearrange("q (t p) -> q t p", t=TILES),
-                    in0=y2[:].rearrange("q (t p) -> q t p", t=TILES),
-                    in1=ms[c][:].rearrange("q (p t) -> q t p", t=TILES),
-                    op=ALU.mult,
-                )
-                gts[(c, jt)] = gt
+            cols = slice(jt * P, (jt + 1) * P)
+            fz = banks[bank].tile([P, CHUNK], F32, tag=bank)
+            nc.tensor.matmul_mx(
+                out=fz[:],
+                lhsT=wf_codes[:, cols].bitcast(FP8X4),
+                lhsT_scale=wf_scl[:, cols],
+                rhs=cd[:].bitcast(FP8X4),
+                rhs_scale=sc[:],
+                start=True,
+                stop=True,
+            )
+            fzs[(c, jt)] = fz
 
+        def fi_y(c, jt):
+            y2 = work.tile([P, CHUNK], F32, tag="y%d" % jt)
+            nc.scalar.activation(
+                out=y2[:], in_=fzs[(c, jt)][:], func=AF.Identity, bias=bf2[:, jt : jt + 1], scale=2.0
+            )
+            ys[(c, jt)] = y2
+
+        def fi_g(c, jt, eng):
+            gt = work.tile([P, CHUNK], F32, tag="g%d" % jt)
+            eng.tensor_tensor(
+                out=gt[:].rearrange("q (t p) -> q t p", t=TILES),
+                in0=ys[(c, jt)][:].rearrange("q (t p) -> q t p", t=TILES),
+                in1=ms[c][:].rearrange("q (p t) -> q t p", t=TILES),
+                op=ALU.mult,
+            )
+            gts[(c, jt)] = gt
+
+        zts = {}
         fts = {}
 
-        def z_half(c, k, jt0):
-            for jt in range(jt0, jt0 + 1):
-                ct = 2 * k + jt
-                cols = slice(ct * P, (ct + 1) * P)
-                zp = zps.tile([P, CHUNK], F32, tag="z")
-                for g in range(2):
-                    cd, sc = codes[(c, 1 + g)]
-                    nc.tensor.matmul_mx(
-                        out=zp[:],
-                        lhsT=w_codes[:, g, cols].bitcast(FP8X4),
-                        lhsT_scale=w_scl[:, g, cols],
-                        rhs=cd[:].bitcast(FP8X4),
-                        rhs_scale=sc[:],
-                        start=(g == 0),
-                        stop=(g == 1),
-                    )
-                u_sb = work.tile([P, CHUNK], F32, tag="u", bufs=4)
-                nc.vector.tensor_tensor(out=u_sb[:], in0=zp[:], in1=gts[(c, jt)][:], op=ALU.add)
-                f_sb = work.tile([P, CHUNK], F32, tag="f", bufs=6)
-                nc.scalar.activation(
-                    out=f_sb[:], in_=u_sb[:], func=AF.Sigmoid, bias=bias[:, ct : ct + 1], scale=1.0
+        def z_pe(c, k, jt):
+            ct = 2 * k + jt
+            cols = slice(ct * P, (ct + 1) * P)
+            zp = zps.tile([P, CHUNK], F32, tag="z")
+            for g in range(2):
+                cd, sc = codes[(c, 1 + g)]
+                nc.tensor.matmul_mx(
+                    out=zp[:],
+                    lhsT=w_codes[:, g, cols].bitcast(FP8X4),
+                    lhsT_scale=w_scl[:, g, cols],
+                    rhs=cd[:].bitcast(FP8X4),
+                    rhs_scale=sc[:],
+                    start=(g == 0),
+                    stop=(g == 1),
                 )
-                fts[(c, ct)] = f_sb
+            zts[(c, ct)] = zp
 
+        def gate(c, k, jt):
+            ct = 2 * k + jt
+            u_sb = work.tile([P, CHUNK], F32, tag="u", bufs=4)
+            nc.vector.tensor_tensor(out=u_sb[:], in0=zts[(c, ct)][:], in1=gts[(c, jt)][:], op=ALU.add)
+            f_sb = work.tile([P, CHUNK], F32, tag="f", bufs=10)
+            nc.scalar.activation(
+                out=f_sb[:], in_=u_sb[:], func=AF.Sigmoid, bias=bias[:, ct : ct + 1], scale=1.0
+            )
+            fts[(c, ct)] = f_sb
+
+        fbs = {}
         prods = {}
-        cur = [None]
         accs = {}
 
-        def fb_half(c, k, hh0):
-            c4 = cs[c][:].rearrange("p (t k j) -> p t k j", t=TILES, k=KIDS)
-            if hh0 == 0:
-                prod = work.tile([P, TILES, HDIM], F32, tag="prod", bufs=3)
-                cur[0] = prod
-            prod = cur[0]
-            last = c == NCHUNK - 1
-            for hh in range(hh0, hh0 + 1):
-                fb = fps.tile([P, 2, HDIM], F32, tag="fb")
-                for tt in range(2):
-                    t = 2 * hh + tt
-                    for jt in range(2):
-                        nc.tensor.transpose(
-                            fb[:, tt, jt * P : (jt + 1) * P],
-                            fts[(c, 2 * k + jt)][:, t * P : (t + 1) * P],
-                            ident[:],
-                        )
-                nc.vector.tensor_tensor(
-                    out=prod[:, 2 * hh : 2 * hh + 2, :],
-                    in0=fb[:],
-                    in1=c4[:, 2 * hh : 2 * hh + 2, k, :],
-                    op=ALU.mult,
-                )
-                if last and k >= 2:
-                    half = slice(2 * hh, 2 * hh + 2)
-                    eng = nc.vector if k == 3 else nc.gpsimd
-                    eng.tensor_tensor(
-                        out=accs[c][:, half, :], in0=accs[c][:, half, :], in1=prod[:, half, :], op=ALU.add
+        def fb_pe(c, k, hh):
+            fb = fps.tile([P, 2, HDIM], F32, tag="fb")
+            for tt in range(2):
+                t = 2 * hh + tt
+                for jt in range(2):
+                    nc.tensor.transpose(
+                        fb[:, tt, jt * P : (jt + 1) * P],
+                        fts[(c, 2 * k + jt)][:, t * P : (t + 1) * P],
+                        ident[:],
                     )
-                    if k == 3:
-                        nc.sync.dma_start(
-                            out=o_v[c][:, hh * 2 * HDIM : (hh + 1) * 2 * HDIM],
-                            in_=accs[c][:, half, :].rearrange("p t j -> p (t j)"),
-                        )
-            if hh0 == 0:
-                return
-            if k == 0:
-                prods[c] = prod
-            elif k == 1:
+            fbs[(c, k, hh)] = fb
+
+        def times_c(c, k, hh):
+            if hh == 0:
+                prod = work.tile([P, TILES, HDIM], F32, tag="prod", bufs=4)
+                prods[(c, k)] = prod
+            half = slice(2 * hh, 2 * hh + 2)
+            c4 = cs[c][:].rearrange("p (t k j) -> p t k j", t=TILES, k=KIDS)
+            nc.vector.tensor_tensor(
+                out=prods[(c, k)][:, half, :], in0=fbs[(c, k, hh)][:], in1=c4[:, half, k, :], op=ALU.mult
+            )
+
+        def finish(c, k):
+            last = c == NCHUNK - 1
+            for hh in range(2):
+                times_c(c, k, hh)
+                if last and k == 3:
+                    half = slice(2 * hh, 2 * hh + 2)
+                    nc.vector.tensor_tensor(
+                        out=prods[(c, 3)][:, half, :],
+                        in0=prods[(c, 3)][:, half, :],
+                        in1=prods[(c, 2)][:, half, :],
+                        op=ALU.add,
+                    )
+                    nc.vector.tensor_tensor(
+                        out=accs[c][:, half, :],
+                        in0=accs[c][:, half, :],
+                        in1=prods[(c, 3)][:, half, :],
+                        op=ALU.add,
+                    )
+                    nc.sync.dma_start(
+                        out=o_v[c][:, hh * 2 * HDIM : (hh + 1) * 2 * HDIM],
+                        in_=accs[c][:, half, :].rearrange("p t j -> p (t j)"),
+                    )
+            if k == 1:
                 acc = work.tile([P, TILES, HDIM], F32, tag="acc")
-                nc.gpsimd.tensor_tensor(out=acc[:], in0=prods[c][:], in1=prod[:], op=ALU.add)
+                nc.gpsimd.tensor_tensor(
+                    out=acc[:], in0=prods[(c, 0)][:], in1=prods[(c, 1)][:], op=ALU.add
+                )
                 accs[c] = acc
-            elif not last:
-                nc.gpsimd.tensor_tensor(out=accs[c][:], in0=accs[c][:], in1=prod[:], op=ALU.add)
-                if k == KIDS - 1:
+            elif k >= 2 and not last:
+                nc.gpsimd.tensor_tensor(
+                    out=accs[c][:], in0=accs[c][:], in1=prods[(c, k)][:], op=ALU.add
+                )
+                if k == 3:
                     nc.sync.dma_start(out=o_v[c], in_=accs[c][:].rearrange("p t j -> p (t j)"))
 
-        tr_unit(0, 0, 0)
-        tr_unit(0, 0, 1)
+        nc.vector.tensor_copy(out=wf_grp[:], in_=wf_raw[:].rearrange("q t c -> q c t"))
+        tr_pe(0, 0, 0, "tp")
+        tr_pe(0, 0, 1, "tp")
+        tr_cp(0, 0, 0, False)
+        tr_cp(0, 0, 1, True)
         nc.vector.quantize_mx(
             out=wf_codes[:].bitcast(FP8X4),
             scales=wf_scl[:],
             in_=wf_grp[:].rearrange("q c t -> q (c t)"),
         )
+        tr_quant(0, 0)
+        tr_pe(0, 1, 0, "fb")
+        tr_pe(0, 1, 1, "fb")
+        tr_pe(0, 2, 0, "z")
+        tr_pe(0, 2, 1, "z")
         bias_ps = tps.tile([P, P], BF16, tag="tp")
         nc.tensor.transpose(bias_ps[:], bias_rows[:], ident_bf[:])
         nc.vector.tensor_copy(out=bias[:, 0:10], in_=bias_ps[:, 0:10])
         nc.vector.tensor_scalar_mul(out=bf2[:], in0=bias[:, 8:10], scalar1=2.0)
-        tr_quant(0, 0)
-        tr_unit(0, 1, 0)
-        tr_unit(0, 1, 1)
-        fi_half(0, 0)
-        fi_half(0, 1)
-        tr_unit(0, 2, 0)
-        tr_unit(0, 2, 1)
-        w_regroup(0, 0, 0)
-        w_regroup(1, 0, 0)
+        tr_cp(0, 1, 0, False)
+        tr_cp(0, 1, 1, True)
+        tr_cp(0, 2, 0, False)
+        tr_cp(0, 2, 1, True)
+        fi_pe(0, 0, "z")
+        fi_pe(0, 1, "z")
+        fi_y(0, 0)
+        fi_y(0, 1)
+        w_regroup(0, 0, True)
+        w_regroup(1, 0, True)
         tr_quant(0, 1)
         w_quant(0, 0)
         w_quant(1, 0)
         tr_quant(0, 2)
-        for cb in range(1, 4):
-            w_regroup(0, cb, 1)
-            w_regroup(1, cb, 1)
+        w_regroup(0, 1, True)
+        w_regroup(1, 1, True)
+        for cb in range(2, 4):
+            w_regroup(0, cb, False)
+            w_regroup(1, cb, False)
+        w_quant(0, 1)
+        w_quant(1, 1)
+        fi_g(0, 0, nc.vector)
+        fi_g(0, 1, nc.vector)
 
-        steps = [(c, k) for c in range(NCHUNK) for k in range(KIDS)]
-        for s, (c, k) in enumerate(steps):
-            more = c + 1 < NCHUNK
-            for half in range(2):
-                if k == 3 and more:
-                    fi_half(c + 1, half)
-                z_half(c, k, half)
-                if c == 0 and k < 3:
-                    w_quant(half, k + 1)
-                if more and k >= 1 and half == 0:
-                    tr_quant(c + 1, k - 1)
-                if k == 0 and half == 0 and c + 2 < NCHUNK:
-                    load_xh(c + 2)
-                if more and k < 3:
-                    tr_unit(c + 1, k, half)
-                if s >= 1:
-                    fb_half(steps[s - 1][0], steps[s - 1][1], half)
-            if k == 0 and c + 2 < NCHUNK:
-                load_c(c + 2)
-        fb_half(NCHUNK - 1, KIDS - 1, 0)
-        fb_half(NCHUNK - 1, KIDS - 1, 1)
+        total = NCHUNK * KIDS
+        for i in range(total + LAG):
+            c, j = divmod(i, KIDS)
+            live = i < total
+            units = []
+            if live:
+                if i == 0:
+                    units.append((1, 0))
+                if j == 0 and c + 1 < NCHUNK:
+                    units.append((c + 1, 1))
+                if j == 1 and c + 1 < NCHUNK:
+                    units.append((c + 1, 2))
+                if j == 3 and c + 2 < NCHUNK:
+                    units.append((c + 2, 0))
+            fi_now = live and j == 2 and c + 1 < NCHUNK
+            if live:
+                z_pe(c, j, 0)
+                z_pe(c, j, 1)
+            if fi_now:
+                fi_pe(c + 1, 0, "tp")
+                fi_pe(c + 1, 1, "tp")
+            for cc, op in units:
+                tr_pe(cc, op, 0, "tp")
+                tr_pe(cc, op, 1, "tp")
+            if i >= LAG:
+                c2, k2 = divmod(i - LAG, KIDS)
+                fb_pe(c2, k2, 0)
+                fb_pe(c2, k2, 1)
+            if live and j == 0:
+                if c + 2 < NCHUNK:
+                    load_h(c + 2)
+                if c + 3 < NCHUNK:
+                    load_x(c + 3)
+                if i == 0:
+                    load_c(2)
+            if fi_now:
+                for jt in range(2):
+                    fi_y(c + 1, jt)
+                    fi_g(c + 1, jt, nc.gpsimd)
+            for cc, op in units:
+                tr_cp(cc, op, 0, False)
+                tr_cp(cc, op, 1, False)
+            if live:
+                gate(c, j, 0)
+                gate(c, j, 1)
+                if c == 0 and j < 2:
+                    w_quant(0, j + 2)
+                    w_quant(1, j + 2)
+                if i == 1:
+                    tr_quant(1, 0)
+                if c + 1 < NCHUNK and j < 3 and i > 0:
+                    tr_quant(c + 1, j)
+            if i >= LAG:
+                c2, k2 = divmod(i - LAG, KIDS)
+                finish(c2, k2)
+                if k2 == 3 and c2 + 3 < NCHUNK:
+                    load_c(c2 + 3)

@@ -113,14 +113,7 @@ def tile_treelstmcell_pa_t_kernel(
             if on_vector:
                 nc.vector.tensor_copy(out=w_grp[:, g, cols, :], in_=src)
             else:
-                nc.gpsimd.tensor_scalar(
-                    out=w_grp[:, g, cols, :],
-                    in0=src,
-                    scalar1=1.0,
-                    scalar2=0.0,
-                    op0=ALU.mult,
-                    op1=ALU.add,
-                )
+                nc.scalar.copy(out=w_grp[:, g, cols, :], in_=src)
 
         def w_quant(g, cb):
             cols = slice(cb * HDIM, (cb + 1) * HDIM)
@@ -385,6 +378,12 @@ def tile_treelstmcell_pa_t_kernel(
             if live:
                 gate(c, j, 0)
                 gate(c, j, 1)
+            if i >= LAG:
+                c2, k2 = divmod(i - LAG, KIDS)
+                finish(c2, k2)
+                if k2 == 3 and c2 + 3 < NCHUNK:
+                    load_c(c2 + 3)
+            if live:
                 if c == 0 and j < 2:
                     w_quant(0, j + 2)
                     w_quant(1, j + 2)
@@ -392,8 +391,3 @@ def tile_treelstmcell_pa_t_kernel(
                     tr_quant(1, 0)
                 if c + 1 < NCHUNK and j < 3 and i > 0:
                     tr_quant(c + 1, j)
-            if i >= LAG:
-                c2, k2 = divmod(i - LAG, KIDS)
-                finish(c2, k2)
-                if k2 == 3 and c2 + 3 < NCHUNK:
-                    load_c(c2 + 3)

from contextlib import ExitStack

import concourse.mybir as mybir
from concourse.masks import make_identity

F32 = mybir.dt.float32
BF16 = mybir.dt.bfloat16
U32 = mybir.dt.uint32
U8 = mybir.dt.uint8
FP8X4 = mybir.dt.float8_e4m3fn_x4
AF = mybir.ActivationFunctionType
ALU = mybir.AluOpType

P = 128
NODES = 4096
XDIM = 512
HDIM = 256
KIDS = 4
KDIM = KIDS * HDIM
CHUNK = 512
TILES = CHUNK // P
NCHUNK = NODES // CHUNK
LAG = 2
FLOPS = 2 * NODES * KDIM * KDIM + 2 * NODES * XDIM * HDIM


def tile_treelstmcell_pa_t_kernel(
    tc, x, x_mask, neighbour_h, neighbour_c, W_f_in, b_f_in, W_aggr_f, b_aggr_f, out
):
    nc = tc.nc
    x_v = x.rearrange("(c p t) k -> c p (t k)", p=P, t=TILES)
    h_v = neighbour_h.rearrange("(c p t) k j -> c p (t k j)", p=P, t=TILES)
    c_v = neighbour_c.rearrange("(c p t) k j -> c p (t k j)", p=P, t=TILES)
    o_v = out.rearrange("(c p t) j -> c p (t j)", p=P, t=TILES)
    w_v = W_aggr_f.rearrange("(s q e) c -> s q e c", s=4, q=P, e=2)
    wf_v = W_f_in.rearrange("(u q e) c -> q u (e c)", u=2, q=P, e=2)

    with ExitStack() as ctx:
        const = ctx.enter_context(tc.tile_pool(name="const", bufs=1))
        loads = ctx.enter_context(tc.tile_pool(name="loads", bufs=3))
        quant = ctx.enter_context(tc.tile_pool(name="quant", bufs=2))
        work = ctx.enter_context(tc.tile_pool(name="work", bufs=2))
        zps = ctx.enter_context(tc.psum_pool(name="zps", bufs=4))
        fps = ctx.enter_context(tc.psum_pool(name="fps", bufs=2))
        tps = ctx.enter_context(tc.psum_pool(name="tps", bufs=2))
        ctx.enter_context(tc.manual_schedule())
        banks = {"z": zps, "fb": fps, "tp": tps}

        xs = {}
        hs = {}
        cs = {}
        ms = {}

        def load_x(c):
            x_sb = loads.tile([P, TILES * XDIM], BF16, tag="x")
            nc.sync.dma_start(out=x_sb[:], in_=x_v[c])
            xs[c] = x_sb
            m_sb = loads.tile([P, CHUNK], BF16, tag="m")
            nc.sync.dma_start(
                out=m_sb[:], in_=x_mask[c * CHUNK : (c + 1) * CHUNK].partition_broadcast(P)
            )
            ms[c] = m_sb

        def load_h(c):
            h_sb = loads.tile([P, TILES * KDIM], BF16, tag="h", bufs=2)
            nc.sync.dma_start(out=h_sb[:], in_=h_v[c])
            hs[c] = h_sb

        def load_c(c):
            c_sb = loads.tile([P, TILES * KDIM], BF16, tag="c")
            nc.sync.dma_start(out=c_sb[:], in_=c_v[c])
            cs[c] = c_sb

        bias_rows = const.tile([P, P], BF16)
        nc.vector.memset(bias_rows[:], 0.0)
        nc.scalar.dma_start(out=bias_rows[0:8, :], in_=b_aggr_f.rearrange("(r q) -> r q", q=P))
        nc.scalar.dma_start(out=bias_rows[8:10, :], in_=b_f_in.rearrange("(r q) -> r q", q=P))

        load_x(0)
        wf_raw = const.tile([P, 4, HDIM], BF16)
        nc.sync.dma_start(out=wf_raw[:].rearrange("q (u e) c -> q u (e c)", u=2), in_=wf_v)
        load_h(0)
        w_raw = const.tile([P, 8, KDIM], BF16)
        for s in range(4):
            nc.sync.dma_start(out=w_raw[:, 2 * s : 2 * s + 2, 0:HDIM], in_=w_v[s][:, :, 0:HDIM])
        for s in range(4):
            nc.sync.dma_start(
                out=w_raw[:, 2 * s : 2 * s + 2, HDIM:KDIM], in_=w_v[s][:, :, HDIM:KDIM]
            )
        load_x(1)
        load_h(1)
        load_c(0)
        load_x(2)
        load_c(1)

        ident = const.tile([P, P], F32)
        make_identity(nc, ident[:])
        ident_bf = const.tile([P, P], BF16)
        make_identity(nc, ident_bf[:])
        bias = const.tile([P, 16], F32)
        bf2 = const.tile([P, 2], F32)

        wf_grp = const.tile([P, HDIM, 4], BF16, align_bytes=64)
        wf_codes = const.tile([P, HDIM], U32, align_bytes=64)
        wf_scl = const.tile([P, HDIM], U8, align_bytes=64)
        w_grp = const.tile([P, 2, KDIM, 4], BF16, align_bytes=64)
        w_codes = const.tile([P, 2, KDIM], U32, align_bytes=64)
        w_scl = const.tile([P, 2, KDIM], U8, align_bytes=64)

        def w_regroup(g, cb, on_vector):
            cols = slice(cb * HDIM, (cb + 1) * HDIM)
            src = w_raw[:, 4 * g : 4 * g + 4, cols].rearrange("q t c -> q c t")
            if on_vector:
                nc.vector.tensor_copy(out=w_grp[:, g, cols, :], in_=src)
            else:
                nc.scalar.copy(out=w_grp[:, g, cols, :], in_=src)

        def w_quant(g, cb):
            cols = slice(cb * HDIM, (cb + 1) * HDIM)
            nc.vector.quantize_mx(
                out=w_codes[:, g, cols].bitcast(FP8X4),
                scales=w_scl[:, g, cols],
                in_=w_grp[:, g, cols, :].rearrange("q c t -> q (c t)"),
            )

        grps = {}
        codes = {}
        tpt = {}

        def tr_pe(c, op, hh, bank):
            if op == 0:
                words = xs[c][:].bitcast(F32)
                wpt = XDIM // 2
                g = 0
            else:
                words = hs[c][:].bitcast(F32)
                wpt = KDIM // 2
                g = op - 1
            tp = banks[bank].tile([P, 2, 2 * P], F32, tag=bank)
            for u in range(2):
                for tt in range(2):
                    col = (2 * hh + tt) * wpt + (2 * g + u) * P
                    nc.tensor.transpose(
                        tp[:, u, tt * P : (tt + 1) * P], words[:, col : col + P], ident[:]
                    )
            tpt[(c, op, hh)] = tp

        def tr_cp(c, op, hh, on_vector):
            if hh == 0:
                grp = quant.tile([P, CHUNK * 4], BF16, tag="grp%d" % op, align_bytes=64)
                grps[(c, op)] = grp
            dst = grps[(c, op)][:].bitcast(F32).rearrange("p (n u) -> p n u", u=2)
            dst = dst[:, hh * 2 * P : (hh + 1) * 2 * P, :]
            src = tpt[(c, op, hh)][:].rearrange("p u n -> p n u")
            if on_vector:
                nc.vector.tensor_copy(out=dst, in_=src)
            else:
                nc.scalar.copy(out=dst, in_=src)

        def tr_quant(c, op):
            cd = quant.tile([P, CHUNK], U32, tag="cd%d" % op, align_bytes=64)
            sc = quant.tile([P, CHUNK], U8, tag="sc%d" % op, align_bytes=64)
            nc.vector.quantize_mx(out=cd[:].bitcast(FP8X4), scales=sc[:], in_=grps[(c, op)][:])
            codes[(c, op)] = (cd, sc)

        fzs = {}
        ys = {}
        gts = {}

        def fi_pe(c, jt, bank):
            cd, sc = codes[(c, 0)]
            cols = slice(jt * P, (jt + 1) * P)
            fz = banks[bank].tile([P, CHUNK], F32, tag=bank)
            nc.tensor.matmul_mx(
                out=fz[:],
                lhsT=wf_codes[:, cols].bitcast(FP8X4),
                lhsT_scale=wf_scl[:, cols],
                rhs=cd[:].bitcast(FP8X4),
                rhs_scale=sc[:],
                start=True,
                stop=True,
            )
            fzs[(c, jt)] = fz

        def fi_y(c, jt):
            y2 = work.tile([P, CHUNK], F32, tag="y%d" % jt)
            nc.scalar.activation(
                out=y2[:], in_=fzs[(c, jt)][:], func=AF.Identity, bias=bf2[:, jt : jt + 1], scale=2.0
            )
            ys[(c, jt)] = y2

        def fi_g(c, jt, eng):
            gt = work.tile([P, CHUNK], F32, tag="g%d" % jt)
            eng.tensor_tensor(
                out=gt[:].rearrange("q (t p) -> q t p", t=TILES),
                in0=ys[(c, jt)][:].rearrange("q (t p) -> q t p", t=TILES),
                in1=ms[c][:].rearrange("q (p t) -> q t p", t=TILES),
                op=ALU.mult,
            )
            gts[(c, jt)] = gt

        zts = {}
        fts = {}

        def z_pe(c, k, jt):
            ct = 2 * k + jt
            cols = slice(ct * P, (ct + 1) * P)
            zp = zps.tile([P, CHUNK], F32, tag="z")
            for g in range(2):
                cd, sc = codes[(c, 1 + g)]
                nc.tensor.matmul_mx(
                    out=zp[:],
                    lhsT=w_codes[:, g, cols].bitcast(FP8X4),
                    lhsT_scale=w_scl[:, g, cols],
                    rhs=cd[:].bitcast(FP8X4),
                    rhs_scale=sc[:],
                    start=(g == 0),
                    stop=(g == 1),
                )
            zts[(c, ct)] = zp

        def gate(c, k, jt):
            ct = 2 * k + jt
            u_sb = work.tile([P, CHUNK], F32, tag="u", bufs=4)
            nc.vector.tensor_tensor(out=u_sb[:], in0=zts[(c, ct)][:], in1=gts[(c, jt)][:], op=ALU.add)
            f_sb = work.tile([P, CHUNK], F32, tag="f", bufs=10)
            nc.scalar.activation(
                out=f_sb[:], in_=u_sb[:], func=AF.Sigmoid, bias=bias[:, ct : ct + 1], scale=1.0
            )
            fts[(c, ct)] = f_sb

        fbs = {}
        prods = {}
        accs = {}

        def fb_pe(c, k, hh):
            fb = fps.tile([P, 2, HDIM], F32, tag="fb")
            for tt in range(2):
                t = 2 * hh + tt
                for jt in range(2):
                    nc.tensor.transpose(
                        fb[:, tt, jt * P : (jt + 1) * P],
                        fts[(c, 2 * k + jt)][:, t * P : (t + 1) * P],
                        ident[:],
                    )
            fbs[(c, k, hh)] = fb

        def times_c(c, k, hh):
            if hh == 0:
                prod = work.tile([P, TILES, HDIM], F32, tag="prod", bufs=4)
                prods[(c, k)] = prod
            half = slice(2 * hh, 2 * hh + 2)
            c4 = cs[c][:].rearrange("p (t k j) -> p t k j", t=TILES, k=KIDS)
            nc.vector.tensor_tensor(
                out=prods[(c, k)][:, half, :], in0=fbs[(c, k, hh)][:], in1=c4[:, half, k, :], op=ALU.mult
            )

        def finish(c, k):
            last = c == NCHUNK - 1
            for hh in range(2):
                times_c(c, k, hh)
                if last and k == 3:
                    half = slice(2 * hh, 2 * hh + 2)
                    nc.vector.tensor_tensor(
                        out=prods[(c, 3)][:, half, :],
                        in0=prods[(c, 3)][:, half, :],
                        in1=prods[(c, 2)][:, half, :],
                        op=ALU.add,
                    )
                    nc.vector.tensor_tensor(
                        out=accs[c][:, half, :],
                        in0=accs[c][:, half, :],
                        in1=prods[(c, 3)][:, half, :],
                        op=ALU.add,
                    )
                    nc.sync.dma_start(
                        out=o_v[c][:, hh * 2 * HDIM : (hh + 1) * 2 * HDIM],
                        in_=accs[c][:, half, :].rearrange("p t j -> p (t j)"),
                    )
            if k == 1:
                acc = work.tile([P, TILES, HDIM], F32, tag="acc")
                nc.gpsimd.tensor_tensor(
                    out=acc[:], in0=prods[(c, 0)][:], in1=prods[(c, 1)][:], op=ALU.add
                )
                accs[c] = acc
            elif k >= 2 and not last:
                nc.gpsimd.tensor_tensor(
                    out=accs[c][:], in0=accs[c][:], in1=prods[(c, k)][:], op=ALU.add
                )
                if k == 3:
                    nc.sync.dma_start(out=o_v[c], in_=accs[c][:].rearrange("p t j -> p (t j)"))

        nc.vector.tensor_copy(out=wf_grp[:], in_=wf_raw[:].rearrange("q t c -> q c t"))
        tr_pe(0, 0, 0, "tp")
        tr_pe(0, 0, 1, "tp")
        tr_cp(0, 0, 0, False)
        tr_cp(0, 0, 1, True)
        nc.vector.quantize_mx(
            out=wf_codes[:].bitcast(FP8X4),
            scales=wf_scl[:],
            in_=wf_grp[:].rearrange("q c t -> q (c t)"),
        )
        tr_quant(0, 0)
        tr_pe(0, 1, 0, "fb")
        tr_pe(0, 1, 1, "fb")
        tr_pe(0, 2, 0, "z")
        tr_pe(0, 2, 1, "z")
        bias_ps = tps.tile([P, P], BF16, tag="tp")
        nc.tensor.transpose(bias_ps[:], bias_rows[:], ident_bf[:])
        nc.vector.tensor_copy(out=bias[:, 0:10], in_=bias_ps[:, 0:10])
        nc.vector.tensor_scalar_mul(out=bf2[:], in0=bias[:, 8:10], scalar1=2.0)
        tr_cp(0, 1, 0, False)
        tr_cp(0, 1, 1, True)
        tr_cp(0, 2, 0, False)
        tr_cp(0, 2, 1, True)
        fi_pe(0, 0, "z")
        fi_pe(0, 1, "z")
        fi_y(0, 0)
        fi_y(0, 1)
        w_regroup(0, 0, True)
        w_regroup(1, 0, True)
        tr_quant(0, 1)
        w_quant(0, 0)
        w_quant(1, 0)
        tr_quant(0, 2)
        w_regroup(0, 1, True)
        w_regroup(1, 1, True)
        for cb in range(2, 4):
            w_regroup(0, cb, False)
            w_regroup(1, cb, False)
        w_quant(0, 1)
        w_quant(1, 1)
        fi_g(0, 0, nc.vector)
        fi_g(0, 1, nc.vector)

        total = NCHUNK * KIDS
        for i in range(total + LAG):
            c, j = divmod(i, KIDS)
            live = i < total
            units = []
            if live:
                if i == 0:
                    units.append((1, 0))
                if j == 0 and c + 1 < NCHUNK:
                    units.append((c + 1, 1))
                if j == 1 and c + 1 < NCHUNK:
                    units.append((c + 1, 2))
                if j == 3 and c + 2 < NCHUNK:
                    units.append((c + 2, 0))
            fi_now = live and j == 2 and c + 1 < NCHUNK
            if live:
                z_pe(c, j, 0)
                z_pe(c, j, 1)
            if fi_now:
                fi_pe(c + 1, 0, "tp")
                fi_pe(c + 1, 1, "tp")
            for cc, op in units:
                tr_pe(cc, op, 0, "tp")
                tr_pe(cc, op, 1, "tp")
            if i >= LAG:
                c2, k2 = divmod(i - LAG, KIDS)
                fb_pe(c2, k2, 0)
                fb_pe(c2, k2, 1)
            if live and j == 0:
                if c + 2 < NCHUNK:
                    load_h(c + 2)
                if c + 3 < NCHUNK:
                    load_x(c + 3)
                if i == 0:
                    load_c(2)
            if fi_now:
                for jt in range(2):
                    fi_y(c + 1, jt)
                    fi_g(c + 1, jt, nc.gpsimd)
            for cc, op in units:
                tr_cp(cc, op, 0, False)
                tr_cp(cc, op, 1, False)
            if live:
                gate(c, j, 0)
                gate(c, j, 1)
            if i >= LAG:
                c2, k2 = divmod(i - LAG, KIDS)
                finish(c2, k2)
                if k2 == 3 and c2 + 3 < NCHUNK:
                    load_c(c2 + 3)
            if live:
                if c == 0 and j < 2:
                    w_quant(0, j + 2)
                    w_quant(1, j + 2)
                if i == 1:
                    tr_quant(1, 0)
                if c + 1 < NCHUNK and j < 3 and i > 0:
                    tr_quant(c + 1, j)
